import numpy as np
import ml_dtypes


def mxq(x, axis, fmt="e4m3"):
    dtype, down = {"e4m3": (ml_dtypes.float8_e4m3fn, 7), "e5m2": (ml_dtypes.float8_e5m2, 14)}[fmt]
    v = np.moveaxis(np.asarray(x, np.float32).astype(ml_dtypes.bfloat16).astype(np.float64), axis, -1)
    blocks = v.reshape(v.shape[:-1] + (-1, 32))
    amax = np.abs(blocks).max(-1, keepdims=True)
    byte = np.maximum(np.where(amax > 0, np.frexp(amax)[1] - 1 + 127, 0) - down, 1)
    scale = np.exp2(byte - 127.0)
    codes = (blocks / scale).astype(np.float32).astype(dtype).astype(np.float64)
    return np.moveaxis((codes * scale).reshape(v.shape), -1, axis)


WIDE = False


def mx_kscale(k):
    if not WIDE:
        return np.ones(k)
    levels = np.array([10, -10, 5, -5, 0])
    a = np.random.permutation(np.resize(levels, k // 512 * 4)).reshape(k // 512, 4)
    idx = np.arange(k)
    return np.exp2(a[idx // 512, idx % 128 // 32])


BF16 = ml_dtypes.bfloat16


def bf(x):
    return np.asarray(x, np.float32).astype(BF16)


def f64(x):
    return np.asarray(x).astype(np.float64)


E2M1 = np.array([0.0, 0.5, 1.0, 1.5, 2.0, 3.0, 4.0, 6.0, -0.0, -0.5, -1.0, -1.5, -2.0, -3.0, -4.0, -6.0])


def pack_weight(w, fmt):
    k, n = w.shape
    w = f64(bf(w)).reshape(k // 32, 32, n)
    amax = np.abs(w).max(1)
    if fmt == "e4m3":
        byte = np.frexp(amax)[1] - 1 + 127 - 7
    else:
        mant, ex = np.frexp(amax / 6.0)
        byte = np.where(mant > 0.5, ex, ex - 1) + 127
    byte = np.clip(np.where(amax > 0, byte, 1), 1, 254)
    scaled = (w * np.exp2(127.0 - byte)[:, None, :]).reshape(k, n).astype(np.float32)
    by_word = np.ascontiguousarray(scaled.reshape(k // 512, 128, 4, n).transpose(0, 1, 3, 2))
    if fmt == "e4m3":
        words = by_word.astype(ml_dtypes.float8_e4m3fn).view(np.uint8)
    else:
        c = by_word.astype(ml_dtypes.float4_e2m1fn).view(np.uint8) & 0xF
        words = c[..., 0::2] | (c[..., 1::2] << 4)
    return np.ascontiguousarray(words), np.ascontiguousarray(byte.astype(np.uint8).reshape(k // 512, 16, n))


def unpack_weight(words, scales, fmt):
    g, p, n, _ = words.shape
    if fmt == "e4m3":
        vals = np.ascontiguousarray(words).view(ml_dtypes.float8_e4m3fn).astype(np.float64)
    else:
        nib = np.empty((g, p, n, 4), np.uint8)
        nib[..., 0::2] = words & 0xF
        nib[..., 1::2] = words >> 4
        vals = E2M1[nib]
    vals = vals * np.repeat(np.exp2(scales.astype(np.float64) - 127.0), 8, axis=1)[..., None]
    return vals.transpose(0, 1, 3, 2).reshape(g * 512, n)

def pack4(w):
    words, scales = pack_weight(w, "e2m1")
    return words.reshape(words.shape[0], 128, -1), scales


def unpack4(words, scales):
    return unpack_weight(words.reshape(words.shape[0], 128, -1, 2), scales, "e2m1")


B, L, C, H, DH, AX = 2, 64, 16384, 16, 96, 3
D3 = DH // AX
HALF = D3 // 2
ROPE_BASE = 10000.0
COORD_MAX = 10.0


def rope_3d(x, coords):
    inv_freq = 1.0 / (ROPE_BASE ** (np.arange(HALF) / HALF))
    ang = coords[..., None] * inv_freq
    cos = np.cos(ang)[:, None]
    sin = np.sin(ang)[:, None]
    xr = x.reshape(B, H, L, AX, D3)
    x1, x2 = xr[..., :HALF], xr[..., HALF:]
    out = np.concatenate([x1 * cos - x2 * sin, x1 * sin + x2 * cos], axis=-1)
    return out.reshape(B, H, L, DH)


def setup_inputs():
    s = mx_kscale(C)
    x_in = bf(np.random.standard_normal((B, L, C)) * s)
    coords = bf(np.random.uniform(size=(B, L, AX)) * COORD_MAX)
    w = np.random.standard_normal((H * DH, C)) * 1.5 / np.sqrt(C) / s
    words, scales = pack4(np.ascontiguousarray(w.T))
    return {"x_in": x_in,
            "coords": coords,
            "w_words": words,
            "w_scales": scales}


def reference(x_in, coords, w_words, w_scales):
    p = mxq(f64(x_in), 2, "e4m3") @ unpack4(w_words, w_scales)
    p = p.reshape(B, L, H, DH).transpose(0, 2, 1, 3)
    return rope_3d(p, f64(coords))

@@ -1,0 +1,200 @@
+import math
+from contextlib import ExitStack
+
+import concourse.mybir as mybir
+from concourse.masks import make_identity
+
+F32 = mybir.dt.float32
+BF16 = mybir.dt.bfloat16
+I32 = mybir.dt.int32
+U32 = mybir.dt.uint32
+U8 = mybir.dt.uint8
+FP8X4 = mybir.dt.float8_e4m3fn_x4
+FP4X4 = mybir.dt.float4_e2m1fn_x4
+ALU = mybir.AluOpType
+ACT = mybir.ActivationFunctionType
+
+P = 128
+BATCH = 2
+TOKENS_PER_BATCH = 64
+K = 16384
+N = 1536
+HEADS = 16
+HEAD = 96
+AXES = 3
+HALF = 16
+ROPE_BASE = 10000.0
+
+K_PASS = 512
+PASSES = K // K_PASS
+BANK = 512
+BANKS = N // BANK
+
+GROUP = 8
+GROUPS = PASSES // GROUP
+RING = 2
+SCALE_ROWS = 4
+WORD_PASSES = 2
+X_CHUNK = 4096
+PAIR = 2
+
+ROUND_MAGIC = 1.5 * 2.0**23
+
+FLOPS = 2 * P * K * N
+
+
+def tile_crossattnrope_pa_k_kernel(tc, x_in, coords, w_words, w_scales, out):
+    nc = tc.nc
+    with ExitStack() as ctx:
+        keep = ctx.enter_context(tc.tile_pool(name="keep", bufs=1))
+        stage = ctx.enter_context(tc.tile_pool(name="stage", bufs=4))
+        rope = ctx.enter_context(tc.tile_pool(name="rope", bufs=2))
+        acc_pool = ctx.enter_context(tc.psum_pool(name="acc", bufs=1))
+        xt_pool = ctx.enter_context(tc.psum_pool(name="xt", bufs=4))
+        ctx.enter_context(tc.manual_schedule())
+
+        ident = keep.tile([P, P], F32, name="ident")
+        x_sb = keep.tile([P, K], BF16, name="x_sb")
+        x_codes = keep.tile([P, PASSES, P], U32, name="x_codes", align_bytes=64)
+        x_scales = keep.tile([P, PASSES, P], U8, name="x_scales", align_bytes=64)
+        words = keep.tile([P, PASSES, 2 * N], U8, name="words", align_bytes=64)
+        planes = keep.tile([P, RING, GROUP, N], U8, name="planes", align_bytes=64)
+        coords_sb = keep.tile([P, AXES], BF16, name="coords_sb")
+        acc = [acc_pool.tile([P, BANK], F32, name="acc%d" % j) for j in range(BANKS)]
+
+        def load_scales(group):
+            slot = group % RING
+            for first in range(0, GROUP, SCALE_ROWS):
+                g0 = group * GROUP + first
+                for b in range(2):
+                    for r in range(4):
+                        nc.sync.dma_start(
+                            out=planes[32 * b + r : P : 64, slot, first : first + SCALE_ROWS, :].bitcast(I32),
+                            in_=w_scales[g0 : g0 + SCALE_ROWS, 4 * b + r : 16 : 8, :]
+                            .rearrange("g q n -> q g n")
+                            .bitcast(I32),
+                        )
+
+        def load_words(g0, passes, byte_cols):
+            nc.sync.dma_start(
+                out=words[:, g0 : g0 + passes, byte_cols].bitcast(I32),
+                in_=w_words[g0 : g0 + passes, :, byte_cols].rearrange("g p c -> p g c").bitcast(I32),
+            )
+
+        def load_group(group):
+            load_scales(group)
+            if group < GROUPS - 1:
+                for g0 in range(group * GROUP, (group + 1) * GROUP, WORD_PASSES):
+                    load_words(g0, WORD_PASSES, slice(0, 2 * N))
+            else:
+                for j in range(BANKS):
+                    for g0 in range(group * GROUP, (group + 1) * GROUP, SCALE_ROWS):
+                        load_words(g0, SCALE_ROWS, slice(2 * BANK * j, 2 * BANK * (j + 1)))
+
+        def multiply(g, j):
+            nc.tensor.matmul_mx(
+                out=acc[j][:],
+                lhsT=x_codes[:, g, :].bitcast(FP8X4),
+                lhsT_scale=x_scales[:, g, :],
+                rhs=words[:, g, 2 * BANK * j : 2 * BANK * (j + 1)].bitcast(FP4X4),
+                rhs_scale=planes[:, (g // GROUP) % RING, g % GROUP, BANK * j : BANK * (j + 1)],
+                start=(g == 0),
+                stop=(g == PASSES - 1),
+            )
+
+        make_identity(nc, ident[:])
+        for slot in range(RING):
+            nc.vector.memset(planes[:, slot].rearrange("p g n -> p (g n)").bitcast(I32), 0)
+        nc.scalar.dma_start(out=coords_sb[:], in_=coords.rearrange("b l a -> (b l) a"))
+        x_flat = x_in.rearrange("b l k -> (b l) k")
+        for c0 in range(0, K, X_CHUNK):
+            nc.sync.dma_start(out=x_sb[:, c0 : c0 + X_CHUNK], in_=x_flat[:, c0 : c0 + X_CHUNK])
+        for group in range(RING):
+            load_group(group)
+
+        x_words = x_sb[:].bitcast(F32)
+
+        def quantise(first_pass, grouped):
+            nc.vector.quantize_mx(
+                out=x_codes[:, first_pass : first_pass + PAIR, :].rearrange("p s r -> p (s r)").bitcast(FP8X4),
+                scales=x_scales[:, first_pass : first_pass + PAIR, :].rearrange("p s r -> p (s r)"),
+                in_=grouped[:],
+            )
+
+        waiting = None
+        for first_pass in range(0, PASSES, PAIR):
+            xt = xt_pool.tile([P, PAIR, 2, P], F32, name="xt")
+            for s in range(PAIR):
+                w0 = (K_PASS // 2) * (first_pass + s)
+                for u in range(2):
+                    nc.tensor.transpose(xt[:, s, u, :], x_words[:, w0 + u : w0 + K_PASS // 2 : 2], ident[:])
+            grouped = stage.tile([P, PAIR * P * 4], BF16, name="grouped", align_bytes=64)
+            grouped_words = grouped[:].bitcast(F32).rearrange("p (s r u) -> p s r u", s=PAIR, u=2)
+            if (first_pass // PAIR) % 2 == 0:
+                nc.scalar.copy(out=grouped_words, in_=xt[:].rearrange("p s u r -> p s r u"))
+            else:
+                nc.vector.tensor_copy(out=grouped_words, in_=xt[:].rearrange("p s u r -> p s r u"))
+            if waiting is not None:
+                quantise(waiting[0], waiting[1])
+            waiting = (first_pass, grouped)
+        quantise(waiting[0], waiting[1])
+
+        turns = keep.tile([P, 2, AXES, HALF], F32, name="turns")
+        whole = keep.tile([P, 2, AXES, HALF], F32, name="whole")
+        for i in range(HALF):
+            inv_freq = ROPE_BASE ** (-i / HALF)
+            nc.vector.tensor_scalar(
+                out=turns[:, 0, :, i], in0=coords_sb[:], scalar1=inv_freq / (2.0 * math.pi), scalar2=None, op0=ALU.mult
+            )
+        nc.vector.tensor_scalar(out=turns[:, 1], in0=turns[:, 0], scalar1=0.25, scalar2=None, op0=ALU.add)
+        nc.vector.tensor_scalar(
+            out=whole[:], in0=turns[:], scalar1=ROUND_MAGIC, scalar2=ROUND_MAGIC, op0=ALU.add, op1=ALU.subtract
+        )
+        nc.vector.tensor_tensor(out=turns[:], in0=turns[:], in1=whole[:], op=ALU.subtract)
+        cos_head = keep.tile([P, AXES, 2, HALF], F32, name="cos_head")
+        sin_head = keep.tile([P, AXES, 2, HALF], F32, name="sin_head")
+        for half in range(2):
+            nc.scalar.activation(out=cos_head[:, :, half, :], in_=turns[:, 1], func=ACT.Sin, scale=2.0 * math.pi)
+            nc.scalar.activation(
+                out=sin_head[:, :, half, :], in_=turns[:, 0], func=ACT.Sin, scale=(1 - 2 * half) * 2.0 * math.pi
+            )
+        cos_all = keep.tile([P, N], F32, name="cos_all")
+        sin_all = keep.tile([P, N], F32, name="sin_all")
+        for table, head_table in ((cos_all, cos_head), (sin_all, sin_head)):
+            nc.vector.tensor_copy(
+                out=table[:].rearrange("p (h f) -> p h f", f=HEAD),
+                in_=head_table[:].rearrange("p a s i -> p (a s i)").unsqueeze(1).to_broadcast([P, HEADS, HEAD]),
+            )
+
+        for group in range(GROUPS - 1):
+            for g in range(group * GROUP, (group + 1) * GROUP):
+                for j in range(BANKS):
+                    multiply(g, j)
+            if group + RING < GROUPS:
+                load_group(group + RING)
+
+        rotated = keep.tile([P, N], F32, name="rotated")
+        stored_heads = 0
+        for j in range(BANKS):
+            for g in range((GROUPS - 1) * GROUP, PASSES):
+                multiply(g, j)
+            cols = slice(BANK * j, BANK * (j + 1))
+            by_cos = rope.tile([P, BANK], F32, name="by_cos")
+            by_sin = rope.tile([P, BANK], F32, name="by_sin")
+            nc.vector.tensor_tensor(out=by_cos[:], in0=acc[j][:], in1=cos_all[:, cols], op=ALU.mult)
+            nc.vector.tensor_tensor(out=by_sin[:], in0=acc[j][:], in1=sin_all[:, cols], op=ALU.mult)
+            own = by_cos[:].rearrange("p (m s i) -> p m s i", s=2, i=HALF)
+            partner = by_sin[:].rearrange("p (m s i) -> p m s i", s=2, i=HALF)
+            result = rotated[:, cols].rearrange("p (m s i) -> p m s i", s=2, i=HALF)
+            for half in range(2):
+                nc.vector.tensor_tensor(
+                    out=result[:, :, half, :], in0=own[:, :, half, :], in1=partner[:, :, 1 - half, :], op=ALU.add
+                )
+            whole_heads = (BANK * (j + 1)) // HEAD
+            for b in range(BATCH):
+                rows = slice(TOKENS_PER_BATCH * b, TOKENS_PER_BATCH * (b + 1))
+                nc.sync.dma_start(
+                    out=out[b, stored_heads:whole_heads].rearrange("h l d -> l h d"),
+                    in_=rotated[rows, HEAD * stored_heads : HEAD * whole_heads].rearrange("p (h d) -> p h d", d=HEAD),
+                )
+            stored_heads = whole_heads

@@ -33,8 +33,9 @@ BANKS = N // BANK
 GROUP = 8
 GROUPS = PASSES // GROUP
 RING = 2
-SCALE_ROWS = 4
+SCALE_ROWS = 8
 WORD_PASSES = 2
+TAIL = 4
 X_CHUNK = 4096
 PAIR = 2
 
@@ -57,54 +58,62 @@ def tile_crossattnrope_pa_k_kernel(tc, x_in, coords, w_words, w_scales, out):
         x_sb = keep.tile([P, K], BF16, name="x_sb")
         x_codes = keep.tile([P, PASSES, P], U32, name="x_codes", align_bytes=64)
         x_scales = keep.tile([P, PASSES, P], U8, name="x_scales", align_bytes=64)
-        words = keep.tile([P, PASSES, 2 * N], U8, name="words", align_bytes=64)
-        planes = keep.tile([P, RING, GROUP, N], U8, name="planes", align_bytes=64)
+        words = [
+            keep.tile([P, WORD_PASSES, 2 * N], U8, name="words%d" % i, align_bytes=64)
+            for i in range((PASSES - TAIL) // WORD_PASSES)
+        ]
+        tail_words = [keep.tile([P, TAIL, 2 * BANK], U8, name="tail_words%d" % j, align_bytes=64) for j in range(BANKS)]
+        planes = [keep.tile([P, GROUP, N], U8, name="planes%d" % s, align_bytes=64) for s in range(RING)]
         coords_sb = keep.tile([P, AXES], BF16, name="coords_sb")
         acc = [acc_pool.tile([P, BANK], F32, name="acc%d" % j) for j in range(BANKS)]
 
         def load_scales(group):
-            slot = group % RING
+            plane = planes[group % RING]
             for first in range(0, GROUP, SCALE_ROWS):
                 g0 = group * GROUP + first
                 for b in range(2):
                     for r in range(4):
                         nc.sync.dma_start(
-                            out=planes[32 * b + r : P : 64, slot, first : first + SCALE_ROWS, :].bitcast(I32),
+                            out=plane[32 * b + r : P : 64, first : first + SCALE_ROWS, :].bitcast(I32),
                             in_=w_scales[g0 : g0 + SCALE_ROWS, 4 * b + r : 16 : 8, :]
                             .rearrange("g q n -> q g n")
                             .bitcast(I32),
                         )
 
-        def load_words(g0, passes, byte_cols):
-            nc.sync.dma_start(
-                out=words[:, g0 : g0 + passes, byte_cols].bitcast(I32),
-                in_=w_words[g0 : g0 + passes, :, byte_cols].rearrange("g p c -> p g c").bitcast(I32),
-            )
-
         def load_group(group):
             load_scales(group)
-            if group < GROUPS - 1:
-                for g0 in range(group * GROUP, (group + 1) * GROUP, WORD_PASSES):
-                    load_words(g0, WORD_PASSES, slice(0, 2 * N))
-            else:
-                for j in range(BANKS):
-                    for g0 in range(group * GROUP, (group + 1) * GROUP, SCALE_ROWS):
-                        load_words(g0, SCALE_ROWS, slice(2 * BANK * j, 2 * BANK * (j + 1)))
+            for g0 in range(group * GROUP, min((group + 1) * GROUP, PASSES - TAIL), WORD_PASSES):
+                nc.sync.dma_start(
+                    out=words[g0 // WORD_PASSES][:].bitcast(I32),
+                    in_=w_words[g0 : g0 + WORD_PASSES].rearrange("g p c -> p g c").bitcast(I32),
+                )
+
+        def load_tail(j):
+            nc.sync.dma_start(
+                out=tail_words[j][:].bitcast(I32),
+                in_=w_words[PASSES - TAIL : PASSES, :, 2 * BANK * j : 2 * BANK * (j + 1)]
+                .rearrange("g p c -> p g c")
+                .bitcast(I32),
+            )
 
         def multiply(g, j):
+            if g < PASSES - TAIL:
+                w_codes = words[g // WORD_PASSES][:, g % WORD_PASSES, 2 * BANK * j : 2 * BANK * (j + 1)]
+            else:
+                w_codes = tail_words[j][:, g - (PASSES - TAIL), :]
             nc.tensor.matmul_mx(
                 out=acc[j][:],
                 lhsT=x_codes[:, g, :].bitcast(FP8X4),
                 lhsT_scale=x_scales[:, g, :],
-                rhs=words[:, g, 2 * BANK * j : 2 * BANK * (j + 1)].bitcast(FP4X4),
-                rhs_scale=planes[:, (g // GROUP) % RING, g % GROUP, BANK * j : BANK * (j + 1)],
+                rhs=w_codes.bitcast(FP4X4),
+                rhs_scale=planes[(g // GROUP) % RING][:, g % GROUP, BANK * j : BANK * (j + 1)],
                 start=(g == 0),
                 stop=(g == PASSES - 1),
             )
 
         make_identity(nc, ident[:])
-        for slot in range(RING):
-            nc.vector.memset(planes[:, slot].rearrange("p g n -> p (g n)").bitcast(I32), 0)
+        for plane in planes:
+            nc.vector.memset(plane[:].rearrange("p g n -> p (g n)").bitcast(I32), 0)
         nc.scalar.dma_start(out=coords_sb[:], in_=coords.rearrange("b l a -> (b l) a"))
         x_flat = x_in.rearrange("b l k -> (b l) k")
         for c0 in range(0, K, X_CHUNK):
@@ -166,17 +175,20 @@ def tile_crossattnrope_pa_k_kernel(tc, x_in, coords, w_words, w_scales, out):
                 in_=head_table[:].rearrange("p a s i -> p (a s i)").unsqueeze(1).to_broadcast([P, HEADS, HEAD]),
             )
 
-        for group in range(GROUPS - 1):
-            for g in range(group * GROUP, (group + 1) * GROUP):
+        for group in range(GROUPS):
+            for g in range(group * GROUP, min((group + 1) * GROUP, PASSES - TAIL)):
                 for j in range(BANKS):
                     multiply(g, j)
             if group + RING < GROUPS:
                 load_group(group + RING)
+            if group + RING == GROUPS - 1:
+                for j in range(BANKS):
+                    load_tail(j)
 
         rotated = keep.tile([P, N], F32, name="rotated")
         stored_heads = 0
         for j in range(BANKS):
-            for g in range((GROUPS - 1) * GROUP, PASSES):
+            for g in range(PASSES - TAIL, PASSES):
                 multiply(g, j)
             cols = slice(BANK * j, BANK * (j + 1))
             by_cos = rope.tile([P, BANK], F32, name="by_cos")

@@ -32,8 +32,6 @@ BANKS = N // BANK
 
 GROUP = 8
 GROUPS = PASSES // GROUP
-RING = 2
-SCALE_ROWS = 8
 WORD_PASSES = 2
 TAIL = 4
 X_CHUNK = 4096
@@ -48,14 +46,10 @@ def tile_crossattnrope_pa_k_kernel(tc, x_in, coords, w_words, w_scales, out):
     nc = tc.nc
     with ExitStack() as ctx:
         keep = ctx.enter_context(tc.tile_pool(name="keep", bufs=1))
-        stage = ctx.enter_context(tc.tile_pool(name="stage", bufs=4))
-        rope = ctx.enter_context(tc.tile_pool(name="rope", bufs=2))
         acc_pool = ctx.enter_context(tc.psum_pool(name="acc", bufs=1))
-        xt_pool = ctx.enter_context(tc.psum_pool(name="xt", bufs=4))
         ctx.enter_context(tc.manual_schedule())
 
         ident = keep.tile([P, P], F32, name="ident")
-        x_sb = keep.tile([P, K], BF16, name="x_sb")
         x_codes = keep.tile([P, PASSES, P], U32, name="x_codes", align_bytes=64)
         x_scales = keep.tile([P, PASSES, P], U8, name="x_scales", align_bytes=64)
         words = [
@@ -63,30 +57,25 @@ def tile_crossattnrope_pa_k_kernel(tc, x_in, coords, w_words, w_scales, out):
             for i in range((PASSES - TAIL) // WORD_PASSES)
         ]
         tail_words = [keep.tile([P, TAIL, 2 * BANK], U8, name="tail_words%d" % j, align_bytes=64) for j in range(BANKS)]
-        planes = [keep.tile([P, GROUP, N], U8, name="planes%d" % s, align_bytes=64) for s in range(RING)]
+        planes = [keep.tile([P, GROUP, N], U8, name="planes%d" % s, align_bytes=64) for s in range(GROUPS)]
         coords_sb = keep.tile([P, AXES], BF16, name="coords_sb")
         acc = [acc_pool.tile([P, BANK], F32, name="acc%d" % j) for j in range(BANKS)]
 
         def load_scales(group):
-            plane = planes[group % RING]
-            for first in range(0, GROUP, SCALE_ROWS):
-                g0 = group * GROUP + first
-                for b in range(2):
-                    for r in range(4):
-                        nc.sync.dma_start(
-                            out=plane[32 * b + r : P : 64, first : first + SCALE_ROWS, :].bitcast(I32),
-                            in_=w_scales[g0 : g0 + SCALE_ROWS, 4 * b + r : 16 : 8, :]
-                            .rearrange("g q n -> q g n")
-                            .bitcast(I32),
-                        )
+            g0 = group * GROUP
+            for b in range(2):
+                for r in range(4):
+                    nc.sync.dma_start(
+                        out=planes[group][32 * b + r : P : 64, :, :].bitcast(I32),
+                        in_=w_scales[g0 : g0 + GROUP, 4 * b + r : 16 : 8, :].rearrange("g q n -> q g n").bitcast(I32),
+                    )
 
-        def load_group(group):
-            load_scales(group)
-            for g0 in range(group * GROUP, min((group + 1) * GROUP, PASSES - TAIL), WORD_PASSES):
-                nc.sync.dma_start(
-                    out=words[g0 // WORD_PASSES][:].bitcast(I32),
-                    in_=w_words[g0 : g0 + WORD_PASSES].rearrange("g p c -> p g c").bitcast(I32),
-                )
+        def load_words(i):
+            g0 = i * WORD_PASSES
+            nc.sync.dma_start(
+                out=words[i][:].bitcast(I32),
+                in_=w_words[g0 : g0 + WORD_PASSES].rearrange("g p c -> p g c").bitcast(I32),
+            )
 
         def load_tail(j):
             nc.sync.dma_start(
@@ -106,7 +95,7 @@ def tile_crossattnrope_pa_k_kernel(tc, x_in, coords, w_words, w_scales, out):
                 lhsT=x_codes[:, g, :].bitcast(FP8X4),
                 lhsT_scale=x_scales[:, g, :],
                 rhs=w_codes.bitcast(FP4X4),
-                rhs_scale=planes[(g // GROUP) % RING][:, g % GROUP, BANK * j : BANK * (j + 1)],
+                rhs_scale=planes[g // GROUP][:, g % GROUP, BANK * j : BANK * (j + 1)],
                 start=(g == 0),
                 stop=(g == PASSES - 1),
             )
@@ -115,38 +104,48 @@ def tile_crossattnrope_pa_k_kernel(tc, x_in, coords, w_words, w_scales, out):
         for plane in planes:
             nc.vector.memset(plane[:].rearrange("p g n -> p (g n)").bitcast(I32), 0)
         nc.scalar.dma_start(out=coords_sb[:], in_=coords.rearrange("b l a -> (b l) a"))
-        x_flat = x_in.rearrange("b l k -> (b l) k")
-        for c0 in range(0, K, X_CHUNK):
-            nc.sync.dma_start(out=x_sb[:, c0 : c0 + X_CHUNK], in_=x_flat[:, c0 : c0 + X_CHUNK])
-        for group in range(RING):
-            load_group(group)
+        x_pools = (tc.tile_pool(name="x_in", bufs=1), tc.tile_pool(name="stage", bufs=4), tc.psum_pool(name="xt", bufs=4))
+        with x_pools[0] as x_pool, x_pools[1] as stage, x_pools[2] as xt_pool:
+            x_sb = x_pool.tile([P, K], BF16, name="x_sb")
+            x_flat = x_in.rearrange("b l k -> (b l) k")
+            for c0 in range(0, K, X_CHUNK):
+                nc.sync.dma_start(out=x_sb[:, c0 : c0 + X_CHUNK], in_=x_flat[:, c0 : c0 + X_CHUNK])
+            for group in range(GROUPS):
+                load_scales(group)
+            for i in range(len(words)):
+                load_words(i)
+            for j in range(BANKS):
+                load_tail(j)
 
-        x_words = x_sb[:].bitcast(F32)
+            x_words = x_sb[:].bitcast(F32)
 
-        def quantise(first_pass, grouped):
-            nc.vector.quantize_mx(
-                out=x_codes[:, first_pass : first_pass + PAIR, :].rearrange("p s r -> p (s r)").bitcast(FP8X4),
-                scales=x_scales[:, first_pass : first_pass + PAIR, :].rearrange("p s r -> p (s r)"),
-                in_=grouped[:],
-            )
+            def quantise(first_pass, grouped):
+                nc.vector.quantize_mx(
+                    out=x_codes[:, first_pass : first_pass + PAIR, :].rearrange("p s r -> p (s r)").bitcast(FP8X4),
+                    scales=x_scales[:, first_pass : first_pass + PAIR, :].rearrange("p s r -> p (s r)"),
+                    in_=grouped[:],
+                )
 
-        waiting = None
-        for first_pass in range(0, PASSES, PAIR):
-            xt = xt_pool.tile([P, PAIR, 2, P], F32, name="xt")
-            for s in range(PAIR):
-                w0 = (K_PASS // 2) * (first_pass + s)
-                for u in range(2):
-                    nc.tensor.transpose(xt[:, s, u, :], x_words[:, w0 + u : w0 + K_PASS // 2 : 2], ident[:])
-            grouped = stage.tile([P, PAIR * P * 4], BF16, name="grouped", align_bytes=64)
-            grouped_words = grouped[:].bitcast(F32).rearrange("p (s r u) -> p s r u", s=PAIR, u=2)
-            if (first_pass // PAIR) % 2 == 0:
-                nc.scalar.copy(out=grouped_words, in_=xt[:].rearrange("p s u r -> p s r u"))
-            else:
-                nc.vector.tensor_copy(out=grouped_words, in_=xt[:].rearrange("p s u r -> p s r u"))
-            if waiting is not None:
-                quantise(waiting[0], waiting[1])
-            waiting = (first_pass, grouped)
-        quantise(waiting[0], waiting[1])
+            waiting = None
+            for first_pass in range(0, PASSES, PAIR):
+                xt = xt_pool.tile([P, PAIR, 2, P], F32, name="xt")
+                for s in range(PAIR):
+                    w0 = (K_PASS // 2) * (first_pass + s)
+                    for u in range(2):
+                        nc.tensor.transpose(xt[:, s, u, :], x_words[:, w0 + u : w0 + K_PASS // 2 : 2], ident[:])
+                grouped = stage.tile([P, PAIR * P * 4], BF16, name="grouped", align_bytes=64)
+                grouped_words = grouped[:].bitcast(F32).rearrange("p (s r u) -> p s r u", s=PAIR, u=2)
+                if (first_pass // PAIR) % 2 == 0:
+                    nc.scalar.copy(out=grouped_words, in_=xt[:].rearrange("p s u r -> p s r u"))
+                else:
+                    nc.vector.tensor_copy(out=grouped_words, in_=xt[:].rearrange("p s u r -> p s r u"))
+                if waiting is not None:
+                    quantise(waiting[0], waiting[1])
+                waiting = (first_pass, grouped)
+            quantise(waiting[0], waiting[1])
+
+        late = ctx.enter_context(tc.tile_pool(name="late", bufs=1))
+        rope = ctx.enter_context(tc.tile_pool(name="rope", bufs=2))
 
         turns = keep.tile([P, 2, AXES, HALF], F32, name="turns")
         whole = keep.tile([P, 2, AXES, HALF], F32, name="whole")
@@ -167,25 +166,19 @@ def tile_crossattnrope_pa_k_kernel(tc, x_in, coords, w_words, w_scales, out):
             nc.scalar.activation(
                 out=sin_head[:, :, half, :], in_=turns[:, 0], func=ACT.Sin, scale=(1 - 2 * half) * 2.0 * math.pi
             )
-        cos_all = keep.tile([P, N], F32, name="cos_all")
-        sin_all = keep.tile([P, N], F32, name="sin_all")
+        cos_all = late.tile([P, N], F32, name="cos_all")
+        sin_all = late.tile([P, N], F32, name="sin_all")
         for table, head_table in ((cos_all, cos_head), (sin_all, sin_head)):
             nc.vector.tensor_copy(
                 out=table[:].rearrange("p (h f) -> p h f", f=HEAD),
                 in_=head_table[:].rearrange("p a s i -> p (a s i)").unsqueeze(1).to_broadcast([P, HEADS, HEAD]),
             )
 
-        for group in range(GROUPS):
-            for g in range(group * GROUP, min((group + 1) * GROUP, PASSES - TAIL)):
-                for j in range(BANKS):
-                    multiply(g, j)
-            if group + RING < GROUPS:
-                load_group(group + RING)
-            if group + RING == GROUPS - 1:
-                for j in range(BANKS):
-                    load_tail(j)
+        for g in range(PASSES - TAIL):
+            for j in range(BANKS):
+                multiply(g, j)
 
-        rotated = keep.tile([P, N], F32, name="rotated")
+        rotated = late.tile([P, N], F32, name="rotated")
         stored_heads = 0
         for j in range(BANKS):
             for g in range(PASSES - TAIL, PASSES):

@@ -30,7 +30,7 @@ PASSES = K // K_PASS
 BANK = 512
 BANKS = N // BANK
 
-GROUP = 8
+GROUP = 16
 GROUPS = PASSES // GROUP
 WORD_PASSES = 2
 TAIL = 4
@@ -63,11 +63,12 @@ def tile_crossattnrope_pa_k_kernel(tc, x_in, coords, w_words, w_scales, out):
 
         def load_scales(group):
             g0 = group * GROUP
-            for b in range(2):
-                for r in range(4):
+            for i in range(8):
+                for q in (i, i + 8):
+                    p = 32 * (q // 4) + q % 4
                     nc.sync.dma_start(
-                        out=planes[group][32 * b + r : P : 64, :, :].bitcast(I32),
-                        in_=w_scales[g0 : g0 + GROUP, 4 * b + r : 16 : 8, :].rearrange("g q n -> q g n").bitcast(I32),
+                        out=planes[group][p : p + 1, :, :].bitcast(I32),
+                        in_=w_scales[g0 : g0 + GROUP, q : q + 1, :].rearrange("g q n -> q g n").bitcast(I32),
                     )
 
         def load_words(i):

@@ -33,7 +33,8 @@ BANKS = N // BANK
 GROUP = 16
 GROUPS = PASSES // GROUP
 WORD_PASSES = 2
-TAIL = 4
+TAIL = 6
+TAIL_PIECES = ((2, 2, 2), (2, 2, 2), (2, 2, 1, 1))
 X_CHUNK = 4096
 PAIR = 2
 
@@ -56,7 +57,20 @@ def tile_crossattnrope_pa_k_kernel(tc, x_in, coords, w_words, w_scales, out):
             keep.tile([P, WORD_PASSES, 2 * N], U8, name="words%d" % i, align_bytes=64)
             for i in range((PASSES - TAIL) // WORD_PASSES)
         ]
-        tail_words = [keep.tile([P, TAIL, 2 * BANK], U8, name="tail_words%d" % j, align_bytes=64) for j in range(BANKS)]
+        tail_words = [
+            [
+                keep.tile([P, n, 2 * BANK], U8, name="tail_words%d_%d" % (j, i), align_bytes=64)
+                for i, n in enumerate(TAIL_PIECES[j])
+            ]
+            for j in range(BANKS)
+        ]
+        tail_place = {}
+        for j in range(BANKS):
+            g = PASSES - TAIL
+            for i, n in enumerate(TAIL_PIECES[j]):
+                for t in range(n):
+                    tail_place[(j, g + t)] = (i, t)
+                g += n
         planes = [keep.tile([P, GROUP, N], U8, name="planes%d" % s, align_bytes=64) for s in range(GROUPS)]
         coords_sb = keep.tile([P, AXES], BF16, name="coords_sb")
         acc = [acc_pool.tile([P, BANK], F32, name="acc%d" % j) for j in range(BANKS)]
@@ -79,18 +93,22 @@ def tile_crossattnrope_pa_k_kernel(tc, x_in, coords, w_words, w_scales, out):
             )
 
         def load_tail(j):
-            nc.sync.dma_start(
-                out=tail_words[j][:].bitcast(I32),
-                in_=w_words[PASSES - TAIL : PASSES, :, 2 * BANK * j : 2 * BANK * (j + 1)]
-                .rearrange("g p c -> p g c")
-                .bitcast(I32),
-            )
+            g0 = PASSES - TAIL
+            for i, n in enumerate(TAIL_PIECES[j]):
+                nc.sync.dma_start(
+                    out=tail_words[j][i][:].bitcast(I32),
+                    in_=w_words[g0 : g0 + n, :, 2 * BANK * j : 2 * BANK * (j + 1)]
+                    .rearrange("g p c -> p g c")
+                    .bitcast(I32),
+                )
+                g0 += n
 
         def multiply(g, j):
             if g < PASSES - TAIL:
                 w_codes = words[g // WORD_PASSES][:, g % WORD_PASSES, 2 * BANK * j : 2 * BANK * (j + 1)]
             else:
-                w_codes = tail_words[j][:, g - (PASSES - TAIL), :]
+                piece, t = tail_place[(j, g)]
+                w_codes = tail_words[j][piece][:, t, :]
             nc.tensor.matmul_mx(
                 out=acc[j][:],
                 lhsT=x_codes[:, g, :].bitcast(FP8X4),

import math
from contextlib import ExitStack

import concourse.mybir as mybir
from concourse.masks import make_identity

F32 = mybir.dt.float32
BF16 = mybir.dt.bfloat16
I32 = mybir.dt.int32
U32 = mybir.dt.uint32
U8 = mybir.dt.uint8
FP8X4 = mybir.dt.float8_e4m3fn_x4
FP4X4 = mybir.dt.float4_e2m1fn_x4
ALU = mybir.AluOpType
ACT = mybir.ActivationFunctionType

P = 128
BATCH = 2
TOKENS_PER_BATCH = 64
K = 16384
N = 1536
HEADS = 16
HEAD = 96
AXES = 3
HALF = 16
ROPE_BASE = 10000.0

K_PASS = 512
PASSES = K // K_PASS
BANK = 512
BANKS = N // BANK

GROUP = 16
GROUPS = PASSES // GROUP
WORD_PASSES = 2
TAIL = 6
TAIL_PIECES = ((2, 2, 2), (2, 2, 2), (2, 2, 1, 1))
X_CHUNK = 4096
PAIR = 2

ROUND_MAGIC = 1.5 * 2.0**23

FLOPS = 2 * P * K * N


def tile_crossattnrope_pa_k_kernel(tc, x_in, coords, w_words, w_scales, out):
    nc = tc.nc
    with ExitStack() as ctx:
        keep = ctx.enter_context(tc.tile_pool(name="keep", bufs=1))
        acc_pool = ctx.enter_context(tc.psum_pool(name="acc", bufs=1))
        ctx.enter_context(tc.manual_schedule())

        ident = keep.tile([P, P], F32, name="ident")
        x_codes = keep.tile([P, PASSES, P], U32, name="x_codes", align_bytes=64)
        x_scales = keep.tile([P, PASSES, P], U8, name="x_scales", align_bytes=64)
        words = [
            keep.tile([P, WORD_PASSES, 2 * N], U8, name="words%d" % i, align_bytes=64)
            for i in range((PASSES - TAIL) // WORD_PASSES)
        ]
        tail_words = [
            [
                keep.tile([P, n, 2 * BANK], U8, name="tail_words%d_%d" % (j, i), align_bytes=64)
                for i, n in enumerate(TAIL_PIECES[j])
            ]
            for j in range(BANKS)
        ]
        tail_place = {}
        for j in range(BANKS):
            g = PASSES - TAIL
            for i, n in enumerate(TAIL_PIECES[j]):
                for t in range(n):
                    tail_place[(j, g + t)] = (i, t)
                g += n
        planes = [keep.tile([P, GROUP, N], U8, name="planes%d" % s, align_bytes=64) for s in range(GROUPS)]
        coords_sb = keep.tile([P, AXES], BF16, name="coords_sb")
        acc = [acc_pool.tile([P, BANK], F32, name="acc%d" % j) for j in range(BANKS)]

        def load_scales(group):
            g0 = group * GROUP
            for i in range(8):
                for q in (i, i + 8):
                    p = 32 * (q // 4) + q % 4
                    nc.sync.dma_start(
                        out=planes[group][p : p + 1, :, :].bitcast(I32),
                        in_=w_scales[g0 : g0 + GROUP, q : q + 1, :].rearrange("g q n -> q g n").bitcast(I32),
                    )

        def load_words(i):
            g0 = i * WORD_PASSES
            nc.sync.dma_start(
                out=words[i][:].bitcast(I32),
                in_=w_words[g0 : g0 + WORD_PASSES].rearrange("g p c -> p g c").bitcast(I32),
            )

        def load_tail(j):
            g0 = PASSES - TAIL
            for i, n in enumerate(TAIL_PIECES[j]):
                nc.sync.dma_start(
                    out=tail_words[j][i][:].bitcast(I32),
                    in_=w_words[g0 : g0 + n, :, 2 * BANK * j : 2 * BANK * (j + 1)]
                    .rearrange("g p c -> p g c")
                    .bitcast(I32),
                )
                g0 += n

        def multiply(g, j):
            if g < PASSES - TAIL:
                w_codes = words[g // WORD_PASSES][:, g % WORD_PASSES, 2 * BANK * j : 2 * BANK * (j + 1)]
            else:
                piece, t = tail_place[(j, g)]
                w_codes = tail_words[j][piece][:, t, :]
            nc.tensor.matmul_mx(
                out=acc[j][:],
                lhsT=x_codes[:, g, :].bitcast(FP8X4),
                lhsT_scale=x_scales[:, g, :],
                rhs=w_codes.bitcast(FP4X4),
                rhs_scale=planes[g // GROUP][:, g % GROUP, BANK * j : BANK * (j + 1)],
                start=(g == 0),
                stop=(g == PASSES - 1),
            )

        make_identity(nc, ident[:])
        for plane in planes:
            nc.vector.memset(plane[:].rearrange("p g n -> p (g n)").bitcast(I32), 0)
        nc.scalar.dma_start(out=coords_sb[:], in_=coords.rearrange("b l a -> (b l) a"))
        x_pools = (tc.tile_pool(name="x_in", bufs=1), tc.tile_pool(name="stage", bufs=4), tc.psum_pool(name="xt", bufs=4))
        with x_pools[0] as x_pool, x_pools[1] as stage, x_pools[2] as xt_pool:
            x_sb = x_pool.tile([P, K], BF16, name="x_sb")
            x_flat = x_in.rearrange("b l k -> (b l) k")
            for c0 in range(0, K, X_CHUNK):
                nc.sync.dma_start(out=x_sb[:, c0 : c0 + X_CHUNK], in_=x_flat[:, c0 : c0 + X_CHUNK])
            for group in range(GROUPS):
                load_scales(group)
            for i in range(len(words)):
                load_words(i)
            for j in range(BANKS):
                load_tail(j)

            x_words = x_sb[:].bitcast(F32)

            def quantise(first_pass, grouped):
                nc.vector.quantize_mx(
                    out=x_codes[:, first_pass : first_pass + PAIR, :].rearrange("p s r -> p (s r)").bitcast(FP8X4),
                    scales=x_scales[:, first_pass : first_pass + PAIR, :].rearrange("p s r -> p (s r)"),
                    in_=grouped[:],
                )

            waiting = None
            for first_pass in range(0, PASSES, PAIR):
                xt = xt_pool.tile([P, PAIR, 2, P], F32, name="xt")
                for s in range(PAIR):
                    w0 = (K_PASS // 2) * (first_pass + s)
                    for u in range(2):
                        nc.tensor.transpose(xt[:, s, u, :], x_words[:, w0 + u : w0 + K_PASS // 2 : 2], ident[:])
                grouped = stage.tile([P, PAIR * P * 4], BF16, name="grouped", align_bytes=64)
                grouped_words = grouped[:].bitcast(F32).rearrange("p (s r u) -> p s r u", s=PAIR, u=2)
                if (first_pass // PAIR) % 2 == 0:
                    nc.scalar.copy(out=grouped_words, in_=xt[:].rearrange("p s u r -> p s r u"))
                else:
                    nc.vector.tensor_copy(out=grouped_words, in_=xt[:].rearrange("p s u r -> p s r u"))
                if waiting is not None:
                    quantise(waiting[0], waiting[1])
                waiting = (first_pass, grouped)
            quantise(waiting[0], waiting[1])

        late = ctx.enter_context(tc.tile_pool(name="late", bufs=1))
        rope = ctx.enter_context(tc.tile_pool(name="rope", bufs=2))

        turns = keep.tile([P, 2, AXES, HALF], F32, name="turns")
        whole = keep.tile([P, 2, AXES, HALF], F32, name="whole")
        for i in range(HALF):
            inv_freq = ROPE_BASE ** (-i / HALF)
            nc.vector.tensor_scalar(
                out=turns[:, 0, :, i], in0=coords_sb[:], scalar1=inv_freq / (2.0 * math.pi), scalar2=None, op0=ALU.mult
            )
        nc.vector.tensor_scalar(out=turns[:, 1], in0=turns[:, 0], scalar1=0.25, scalar2=None, op0=ALU.add)
        nc.vector.tensor_scalar(
            out=whole[:], in0=turns[:], scalar1=ROUND_MAGIC, scalar2=ROUND_MAGIC, op0=ALU.add, op1=ALU.subtract
        )
        nc.vector.tensor_tensor(out=turns[:], in0=turns[:], in1=whole[:], op=ALU.subtract)
        cos_head = keep.tile([P, AXES, 2, HALF], F32, name="cos_head")
        sin_head = keep.tile([P, AXES, 2, HALF], F32, name="sin_head")
        for half in range(2):
            nc.scalar.activation(out=cos_head[:, :, half, :], in_=turns[:, 1], func=ACT.Sin, scale=2.0 * math.pi)
            nc.scalar.activation(
                out=sin_head[:, :, half, :], in_=turns[:, 0], func=ACT.Sin, scale=(1 - 2 * half) * 2.0 * math.pi
            )
        cos_all = late.tile([P, N], F32, name="cos_all")
        sin_all = late.tile([P, N], F32, name="sin_all")
        for table, head_table in ((cos_all, cos_head), (sin_all, sin_head)):
            nc.vector.tensor_copy(
                out=table[:].rearrange("p (h f) -> p h f", f=HEAD),
                in_=head_table[:].rearrange("p a s i -> p (a s i)").unsqueeze(1).to_broadcast([P, HEADS, HEAD]),
            )

        for g in range(PASSES - TAIL):
            for j in range(BANKS):
                multiply(g, j)

        rotated = late.tile([P, N], F32, name="rotated")
        stored_heads = 0
        for j in range(BANKS):
            for g in range(PASSES - TAIL, PASSES):
                multiply(g, j)
            cols = slice(BANK * j, BANK * (j + 1))
            by_cos = rope.tile([P, BANK], F32, name="by_cos")
            by_sin = rope.tile([P, BANK], F32, name="by_sin")
            nc.vector.tensor_tensor(out=by_cos[:], in0=acc[j][:], in1=cos_all[:, cols], op=ALU.mult)
            nc.vector.tensor_tensor(out=by_sin[:], in0=acc[j][:], in1=sin_all[:, cols], op=ALU.mult)
            own = by_cos[:].rearrange("p (m s i) -> p m s i", s=2, i=HALF)
            partner = by_sin[:].rearrange("p (m s i) -> p m s i", s=2, i=HALF)
            result = rotated[:, cols].rearrange("p (m s i) -> p m s i", s=2, i=HALF)
            for half in range(2):
                nc.vector.tensor_tensor(
                    out=result[:, :, half, :], in0=own[:, :, half, :], in1=partner[:, :, 1 - half, :], op=ALU.add
                )
            whole_heads = (BANK * (j + 1)) // HEAD
            for b in range(BATCH):
                rows = slice(TOKENS_PER_BATCH * b, TOKENS_PER_BATCH * (b + 1))
                nc.sync.dma_start(
                    out=out[b, stored_heads:whole_heads].rearrange("h l d -> l h d"),
                    in_=rotated[rows, HEAD * stored_heads : HEAD * whole_heads].rearrange("p (h d) -> p h d", d=HEAD),
                )
            stored_heads = whole_heads
